import numpy as np
import ml_dtypes


def mxq(x, axis, fmt="e4m3"):
    dtype, down = {"e4m3": (ml_dtypes.float8_e4m3fn, 7), "e5m2": (ml_dtypes.float8_e5m2, 14)}[fmt]
    v = np.moveaxis(np.asarray(x, np.float32).astype(ml_dtypes.bfloat16).astype(np.float64), axis, -1)
    blocks = v.reshape(v.shape[:-1] + (-1, 32))
    amax = np.abs(blocks).max(-1, keepdims=True)
    byte = np.maximum(np.where(amax > 0, np.frexp(amax)[1] - 1 + 127, 0) - down, 1)
    scale = np.exp2(byte - 127.0)
    codes = (blocks / scale).astype(np.float32).astype(dtype).astype(np.float64)
    return np.moveaxis((codes * scale).reshape(v.shape), -1, axis)


WIDE = False


def mx_kscale(k):
    if not WIDE:
        return np.ones(k)
    levels = np.array([10, -10, 5, -5, 0])
    if k % 512:
        return np.exp2(np.random.permutation(np.resize(levels, k // 32))).repeat(32)
    a = np.empty((k // 512, 16))
    for p in range(k // 512):
        a[p, :8] = np.random.permutation(np.resize(levels, 8))
        for g in range(8):
            far = levels[np.abs(levels - a[p, g]) >= 10]
            a[p, g + 8] = far[np.random.randint(len(far))]
    return np.exp2(a.ravel()).repeat(32)


BF16 = ml_dtypes.bfloat16


def bf(x):
    return np.asarray(x, np.float32).astype(BF16)


def f64(x):
    return np.asarray(x).astype(np.float64)


B, L, N, RS, D, H, A, F = 4, 4, 128, 16, 512, 8, 64, 2048
S = L * (N + RS)
EPS = 1e-05


def rmsnorm(x, w):
    return x / np.sqrt(np.mean(x * x, -1, keepdims=True) + EPS) * w


def silu(v):
    return v / (1.0 + np.exp(-v))


def draw0():
    s, t = mx_kscale(D), mx_kscale(D)
    return {'o_attn': bf(np.random.standard_normal((B, S, D)) * 0.14 * s),
            'xm': bf(np.random.standard_normal((B, S, D))),
            'attn_o_w': bf(np.random.standard_normal((D, D)) * 3.0 / np.sqrt(D) / s[:, None]),
            'ffn_norm_w': bf((1.0 + 0.1 * np.random.standard_normal(D)) * t),
            'ffn_up_w': bf(np.random.standard_normal((D, 2 * F)) / np.sqrt(D) / t[:, None])}


def core(o_attn, xm, attn_o_w, ffn_norm_w, ffn_up_w):
    x2 = (mxq(f64(o_attn), 2, 'e4m3') @ mxq(f64(attn_o_w), 0, 'e4m3')) + f64(xm)
    xn2 = rmsnorm(x2, f64(ffn_norm_w))
    u1, u2 = np.split(mxq(xn2, 2, 'e4m3') @ mxq(f64(ffn_up_w), 0, 'e4m3'), 2, axis=-1)
    return x2, silu(u1) * u2


def e4m3fn_bytes(y):
    return np.clip(np.asarray(y, np.float64), -448.0, 448.0).astype(np.float32).astype(ml_dtypes.float8_e4m3fn).view(np.uint8)


def e4m3fn_values(b):
    return np.asarray(b, np.uint8).view(ml_dtypes.float8_e4m3fn).astype(np.float64)


def setup_inputs():
    d = draw0()
    x0 = np.asarray(d['ffn_up_w']).astype(np.float64)
    s = (np.max(np.abs(x0), axis=(1,), keepdims=True) / 448.0).astype(np.float32)
    out = {}
    for k, v in d.items():
        if k == 'ffn_up_w':
            out['ffn_up_w_bytes'] = e4m3fn_bytes(x0 / s.astype(np.float64))
            out['ffn_up_w_scale'] = s
        else:
            out[k] = v
    return out


def reference(o_attn, xm, attn_o_w, ffn_norm_w, ffn_up_w_bytes, ffn_up_w_scale):
    return core(o_attn, xm, attn_o_w, ffn_norm_w, e4m3fn_values(ffn_up_w_bytes) * ffn_up_w_scale.astype(np.float64))

from contextlib import ExitStack

import concourse.mybir as mybir
from concourse.masks import make_identity

TOKENS, D, UP, F = 2304, 512, 4096, 2048
EPS = 1e-05
FLOPS = 2 * TOKENS * D * (D + UP)

F32 = mybir.dt.float32
BF16 = mybir.dt.bfloat16
U32 = mybir.dt.uint32
U8 = mybir.dt.uint8
FP8 = mybir.dt.float8_e4m3fn
FP8X4 = mybir.dt.float8_e4m3fn_x4
ACT = mybir.ActivationFunctionType
ALU = mybir.AluOpType

P = 128
TILES = TOKENS // P
PAIRS = TILES // 2
UNIT = 1024


def tile_model_pb_kernel(tc, o_attn, xm, attn_o_w, ffn_norm_w, w_bytes, w_scale, out_0, out_1):
    nc = tc.nc
    o_hbm = o_attn.flatten_outer_dims().rearrange("(p i) d -> p i d", i=TILES)
    xm_hbm = xm.flatten_outer_dims().rearrange("(p i) d -> p i d", i=TILES)
    x2_hbm = out_0.flatten_outer_dims().rearrange("(p i) d -> p i d", i=TILES)
    h_hbm = out_1.flatten_outer_dims().rearrange("(p i) f -> p i f", i=TILES)
    wb_hbm = w_bytes.rearrange("(p t) (v n) -> p (t v) n", t=4, v=2)

    with ExitStack() as ctx:
        keep = ctx.enter_context(tc.tile_pool(name="keep", bufs=1))
        pool2 = ctx.enter_context(tc.tile_pool(name="pool2", bufs=2))
        pool3 = ctx.enter_context(tc.tile_pool(name="pool3", bufs=3))
        pool4 = ctx.enter_context(tc.tile_pool(name="pool4", bufs=4))
        pool5 = ctx.enter_context(tc.tile_pool(name="pool5", bufs=5))
        psum3 = ctx.enter_context(tc.psum_pool(name="psum3", bufs=3))
        psum2 = ctx.enter_context(tc.psum_pool(name="psum2", bufs=2))
        ctx.enter_context(tc.manual_schedule())

        warm = keep.tile([P, 1], F32, name="warm")
        nc.vector.memset(warm[:], 0.0)
        nc.scalar.activation(out=warm[:], in_=warm[:], func=ACT.Silu)
        neg_half = keep.tile([P, 2], F32, name="neg_half")
        nc.gpsimd.memset(neg_half[:], -0.5)
        ident = keep.tile([P, P], F32, name="ident")
        make_identity(nc, ident[:])

        ws = keep.tile([P, 4], F32, name="ws")
        gain = keep.tile([P, D], BF16, name="gain")
        wo_raw = keep.tile([P, 4, D], BF16, name="wo_raw")
        wb = [keep.tile([P, 8, 512], U8, name="wb%d" % k) for k in range(4)]
        groups = [(0, 2), (2, 4), (4, 10), (10, 18)]
        o_sb = [keep.tile([P, b - a, D], BF16, name="o_sb%d" % a, align_bytes=64) for a, b in groups]
        xm_sb = [keep.tile([P, b - a, D], BF16, name="xm_sb%d" % a) for a, b in groups]

        def load_group(which, k):
            a, b = groups[k]
            if which == "o":
                nc.sync.dma_start(out=o_sb[k][:], in_=o_hbm[:, a:b, :])
            else:
                nc.sync.dma_start(out=xm_sb[k][:], in_=xm_hbm[:, a:b, :])

        def group_tile(tiles, i):
            for k, (a, b) in enumerate(groups):
                if a <= i < b:
                    return tiles[k][:, i - a, :]

        def load_unit(j):
            nc.sync.dma_start(out=wb[j][:], in_=wb_hbm[:, :, j * 512 : j * 512 + 512])

        nc.sync.dma_start(out=ws[:], in_=w_scale.rearrange("(p t) o -> p (t o)", t=4))
        load_unit(0)
        load_group("o", 0)
        nc.sync.dma_start(out=wo_raw[:], in_=attn_o_w.rearrange("(p t) n -> p t n", t=4))
        load_group("xm", 0)
        load_unit(1)
        nc.sync.dma_start(out=gain[:], in_=ffn_norm_w.partition_broadcast(P))
        load_group("o", 1)
        load_group("xm", 1)
        load_group("o", 2)
        load_unit(2)
        load_unit(3)
        load_group("xm", 2)
        load_group("o", 3)
        load_group("xm", 3)

        wo_codes = keep.tile([P, D], U32, name="wo_codes", align_bytes=64)
        wo_scales = keep.tile([P, D], U8, name="wo_scales", align_bytes=64)
        w_codes = [keep.tile([P, 512], U32, name="w_codes%d" % k, align_bytes=64) for k in range(8)]
        w_scales = [keep.tile([P, 512], U8, name="w_scales%d" % k, align_bytes=64) for k in range(8)]
        wo_grp = keep.tile([P, D, 4], BF16, name="wo_grp", align_bytes=64)
        wide = {}
        wgrp = {}

        def widen(k, t):
            if k not in wide:
                wide[k] = pool3.tile([P, 4, UNIT], BF16, name="wide")
            nc.vector.tensor_scalar(
                out=wide[k][:, t, :], in0=wb[k][:, 2 * t : 2 * t + 2, :].rearrange("p v n -> p (v n)").bitcast(FP8),
                scalar1=ws[:, t : t + 1], scalar2=None, op0=ALU.mult)

        def interleave(k, half, eng):
            g = pool3.tile([P, 2048], BF16, name="wgrp", align_bytes=64)
            wgrp[k, half] = g
            dst = g[:].rearrange("p (c i t) -> p c t i", i=4, t=4)
            src = wide[k][:, :, 512 * half : 512 * half + 512].rearrange("p t (c i) -> p c t i", i=4)
            if eng == "S":
                nc.scalar.copy(out=dst, in_=src)
            else:
                nc.vector.tensor_copy(out=dst, in_=src)

        def quant_w(j, up):
            nc.vector.quantize_mx(out=w_codes[2 * j + up][:].bitcast(FP8X4), scales=w_scales[2 * j + up][:], in_=wgrp[j, up][:])

        def interleave_wo():
            nc.scalar.copy(out=wo_grp[:].rearrange("p (c i) t -> p c t i", i=4), in_=wo_raw[:].rearrange("p t (c i) -> p c t i", i=4))

        def quant_wo():
            nc.vector.quantize_mx(out=wo_codes[:].bitcast(FP8X4), scales=wo_scales[:],
                                  in_=wo_grp[:].rearrange("p n t -> p (n t)"))

        st = {}

        def transpose_o(g):
            bank = psum2.tile([P, 2, 2, P], F32, name="misc")
            st["to", g] = bank
            for i in range(2):
                words = group_tile(o_sb, 2 * g + i).bitcast(F32)
                for u in range(2):
                    nc.tensor.transpose(bank[:, i, u, :], words[:, u:256:2], ident[:])

        def transpose_x(g):
            bank = psum2.tile([P, 2, 2, P], F32, name="misc")
            st["tx", g] = bank
            for i in range(2):
                words = st["xn", g][:, i, :].bitcast(F32)
                for u in range(2):
                    nc.tensor.transpose(bank[:, i, u, :], words[:, u:256:2], ident[:])

        def copy_t(kind, g):
            raw = pool4.tile([P, 1024], BF16, name="raw_" + kind, align_bytes=64)
            st["raw" + kind, g] = raw
            nc.scalar.copy(out=raw[:].bitcast(F32).rearrange("p (i r u) -> p i r u", i=2, u=2),
                           in_=st["t" + kind, g][:].rearrange("p i u r -> p i r u"))

        def quant_t(kind, g):
            pool = pool4
            codes = pool.tile([P, 256], U32, name="codes_" + kind, align_bytes=64)
            scales = pool.tile([P, 256], U8, name="scales_" + kind, align_bytes=64)
            st["q" + kind, g] = (codes, scales)
            nc.vector.quantize_mx(out=codes[:].bitcast(FP8X4), scales=scales[:], in_=st["raw" + kind, g][:])

        def mm1(g, i):
            codes, scales = st["qo", g]
            acc = psum2.tile([P, D], F32, name="misc")
            st["acc", g, i] = acc
            nc.tensor.matmul_mx(out=acc[:], lhsT=codes[:, i * P : (i + 1) * P].bitcast(FP8X4),
                                lhsT_scale=scales[:, i * P : (i + 1) * P],
                                rhs=wo_codes[:].bitcast(FP8X4), rhs_scale=wo_scales[:], start=True, stop=True)

        def add(g, i):
            if ("x2", g) not in st:
                x2_new = pool4.tile([P, 2, D], F32, name="x2")
                st["x2", g] = x2_new
            x2 = st["x2", g]
            nc.vector.tensor_tensor(out=x2[:, i, :], in0=st["acc", g, i][:], in1=group_tile(xm_sb, 2 * g + i), op=ALU.add)
            if i == 1:
                nc.sync.dma_start(out=x2_hbm[:, 2 * g : 2 * g + 2, :], in_=x2[:])

        def square(g, i):
            if ("ss", g) not in st:
                ss_new = pool3.tile([P, 2], F32, name="ss")
                st["ss", g] = ss_new
            junk = pool2.tile([P, D], BF16, name="junk")
            nc.scalar.activation(out=junk[:], in_=st["x2", g][:, i, :], func=ACT.Square, accum_out=st["ss", g][:, i : i + 1])
            if i == 1:
                ms = pool3.tile([P, 2], F32, name="ms")
                rstd = pool3.tile([P, 2], F32, name="rstd")
                st["rstd", g] = rstd
                nc.gpsimd.tensor_scalar(out=ms[:], in0=st["ss", g][:], scalar1=1.0 / D, scalar2=EPS, op0=ALU.mult, op1=ALU.add)
                nc.gpsimd.tensor_tensor(out=rstd[:], in0=ms[:], in1=neg_half[:], op=ALU.pow)

        def norm(g, i):
            if ("xn", g) not in st:
                xn_new = pool4.tile([P, 2, D], BF16, name="xn", align_bytes=64)
                st["xn", g] = xn_new
            nc.vector.scalar_tensor_tensor(out=st["xn", g][:, i, :], in0=st["x2", g][:, i, :], scalar=st["rstd", g][:, i : i + 1],
                                           in1=gain[:], op0=ALU.mult, op1=ALU.mult)

        def mm2(i, j):
            codes, scales = st["qx", i // 2]
            cols = slice((i % 2) * P, (i % 2) * P + P)
            for up in range(2):
                c = 2 * j + up
                bank = psum3.tile([P, 512], F32, name="u%d" % up)
                st["u", i, j, up] = bank
                nc.tensor.matmul_mx(out=bank[:], lhsT=codes[:, cols].bitcast(FP8X4), lhsT_scale=scales[:, cols],
                                    rhs=w_codes[c][:].bitcast(FP8X4), rhs_scale=w_scales[c][:], start=True, stop=True)

        def silu(i, j):
            gate = pool4.tile([P, 512], F32, name="gate")
            st["gate", i, j] = gate
            nc.scalar.activation(out=gate[:], in_=st["u", i, j, 0][:], func=ACT.Silu)

        def mul(i, j):
            if ("h", i) not in st:
                h_new = pool5.tile([P, F], F32, name="h")
                st["h", i] = h_new
            cols = slice(j * 512, j * 512 + 512)
            h = st["h", i]
            nc.vector.tensor_tensor(out=h[:, cols], in0=st["u", i, j, 1][:], in1=st["gate", i, j][:], op=ALU.mult)
            if i == TILES - 1:
                nc.sync.dma_start(out=h_hbm[:, i, cols], in_=h[:, cols])
            elif j == 3:
                nc.sync.dma_start(out=h_hbm[:, i, :], in_=h[:])

        widen(0, 2)
        widen(0, 0)
        transpose_o(0)
        widen(0, 3)
        copy_t("o", 0)
        widen(0, 1)
        interleave_wo()
        quant_t("o", 0)
        widen(1, 1)
        widen(1, 3)
        interleave(0, 0, "S")
        transpose_o(1)
        quant_wo()
        widen(1, 0)
        mm1(0, 0)
        add(0, 0)
        copy_t("o", 1)
        interleave(0, 1, "S")
        mm1(0, 1)
        transpose_o(2)
        widen(2, 3)
        widen(2, 2)
        add(0, 1)
        widen(2, 1)
        copy_t("o", 2)
        transpose_o(3)
        widen(3, 0)
        square(0, 0)
        transpose_o(4)
        widen(3, 1)
        square(0, 1)
        quant_w(0, 1)
        copy_t("o", 3)
        widen(2, 0)
        copy_t("o", 4)
        norm(0, 0)
        interleave(2, 1, "S")
        norm(0, 1)
        transpose_x(0)
        widen(3, 2)
        transpose_o(5)
        widen(1, 2)
        quant_t("o", 1)
        copy_t("x", 0)
        quant_w(0, 0)
        copy_t("o", 5)
        quant_w(2, 1)
        mm1(1, 1)
        interleave(1, 0, "S")
        mm1(1, 0)
        quant_t("x", 0)
        quant_t("o", 2)
        mm2(0, 0)
        add(1, 0)
        mm2(1, 0)
        add(1, 1)
        widen(3, 3)
        mm1(2, 0)
        mm1(2, 1)
        interleave(1, 1, "S")
        quant_w(1, 0)
        add(2, 0)
        add(2, 1)
        quant_t("o", 3)
        quant_t("o", 4)
        mm1(3, 0)
        square(1, 0)
        quant_w(1, 1)
        mm1(4, 0)
        square(1, 1)
        mm2(0, 1)
        add(3, 0)
        interleave(3, 0, "S")
        add(4, 0)
        mm1(3, 1)
        norm(1, 1)
        mm1(4, 1)
        add(3, 1)
        quant_t("o", 5)
        transpose_o(6)
        add(4, 1)
        interleave(3, 1, "S")
        quant_w(3, 0)
        mm1(5, 0)
        silu(0, 0)
        quant_w(3, 1)
        silu(1, 0)
        mul(0, 0)
        mm2(1, 1)
        silu(0, 1)
        mul(1, 0)
        copy_t("o", 6)
        mul(0, 1)
        square(2, 0)
        mm1(5, 1)
        norm(1, 0)
        square(2, 1)
        add(5, 0)
        silu(1, 1)
        quant_t("o", 6)
        transpose_x(1)
        add(5, 1)
        square(3, 0)
        norm(2, 0)
        square(3, 1)
        mm1(6, 0)
        norm(2, 1)
        copy_t("x", 1)
        mul(1, 1)
        interleave(2, 0, "S")
        transpose_x(2)
        quant_t("x", 1)
        norm(3, 0)
        mm2(2, 0)
        norm(3, 1)
        mm2(3, 0)
        add(6, 0)
        mm2(2, 1)
        silu(2, 0)
        quant_w(2, 0)
        transpose_x(3)
        silu(3, 0)
        mul(2, 0)
        mm2(3, 1)
        copy_t("x", 2)
        mul(3, 0)
        silu(2, 1)
        mm2(0, 2)
        quant_t("x", 2)
        silu(3, 1)
        mm1(6, 1)
        mul(2, 1)
        mm2(1, 2)
        copy_t("x", 3)
        mul(3, 1)
        silu(0, 2)
        mm2(2, 2)
        add(6, 1)
        silu(1, 2)
        transpose_o(7)
        mul(0, 2)
        silu(2, 2)
        mm2(3, 2)
        mul(1, 2)
        copy_t("o", 7)
        mul(2, 2)
        mm2(0, 3)
        silu(3, 2)
        quant_t("o", 7)
        mm2(1, 3)
        silu(0, 3)
        mul(3, 2)
        mm1(7, 0)
        mm1(7, 1)
        silu(1, 3)
        mul(0, 3)
        mm2(2, 3)
        square(4, 0)
        mul(1, 3)
        mm2(3, 3)
        silu(2, 3)
        add(7, 0)
        mm2(4, 0)
        silu(3, 3)
        mul(2, 3)
        mm2(4, 1)
        square(4, 1)
        mul(3, 3)
        silu(4, 0)
        mm2(4, 2)
        quant_t("x", 3)
        add(7, 1)
        silu(4, 1)
        transpose_o(8)
        norm(4, 0)
        silu(4, 2)
        mul(4, 0)
        mm2(4, 3)
        square(5, 0)
        norm(4, 1)
        silu(4, 3)
        transpose_x(4)
        mul(4, 1)
        square(5, 1)
        mm2(5, 0)
        mul(4, 2)
        copy_t("o", 8)
        mul(4, 3)
        mm2(5, 1)
        copy_t("x", 4)
        norm(5, 0)
        mm2(5, 2)
        silu(5, 0)
        quant_t("o", 8)
        silu(5, 1)
        mul(5, 0)
        mm2(5, 3)
        silu(5, 2)
        mul(5, 1)
        silu(5, 3)
        mm1(8, 0)
        mul(5, 2)
        mm1(8, 1)
        square(6, 0)
        mm2(6, 0)
        mul(5, 3)
        square(6, 1)
        mm2(6, 1)
        add(8, 0)
        silu(6, 0)
        mm2(6, 2)
        add(8, 1)
        silu(6, 1)
        norm(6, 0)
        silu(6, 2)
        mul(6, 0)
        mm2(6, 3)
        silu(6, 3)
        mul(6, 1)
        square(7, 0)
        mm2(7, 0)
        mul(6, 2)
        square(8, 0)
        mm2(7, 1)
        norm(5, 1)
        silu(7, 0)
        transpose_x(5)
        quant_t("x", 4)
        silu(7, 1)
        mul(6, 3)
        mm2(7, 2)
        copy_t("x", 5)
        mul(7, 0)
        mm2(7, 3)
        silu(7, 2)
        mul(7, 1)
        mm2(8, 0)
        silu(7, 3)
        quant_t("x", 5)
        mul(7, 2)
        mm2(8, 1)
        silu(8, 0)
        mul(7, 3)
        square(7, 1)
        mm2(8, 2)
        mul(8, 0)
        silu(8, 1)
        mm2(8, 3)
        norm(6, 1)
        silu(8, 2)
        transpose_x(6)
        mul(8, 1)
        silu(8, 3)
        mm2(9, 0)
        mul(8, 2)
        copy_t("x", 6)
        norm(7, 0)
        mm2(9, 1)
        silu(9, 0)
        mul(8, 3)
        mm2(9, 2)
        silu(9, 1)
        mul(9, 0)
        silu(9, 2)
        mm2(9, 3)
        mul(9, 1)
        square(8, 1)
        mm2(10, 0)
        mul(9, 2)
        silu(9, 3)
        mm2(10, 1)
        quant_t("x", 6)
        silu(10, 0)
        mul(9, 3)
        mm2(10, 2)
        silu(10, 1)
        mul(10, 0)
        silu(10, 2)
        mm2(10, 3)
        mul(10, 1)
        silu(10, 3)
        mm2(11, 0)
        mul(10, 2)
        silu(11, 0)
        mm2(11, 1)
        mul(10, 3)
        silu(11, 1)
        mm2(11, 2)
        mul(11, 0)
        silu(11, 2)
        mm2(11, 3)
        mul(11, 1)
        silu(11, 3)
        mm2(12, 0)
        mul(11, 2)
        silu(12, 0)
        mm2(12, 1)
        norm(7, 1)
        silu(12, 1)
        transpose_x(7)
        mul(11, 3)
        mm2(12, 2)
        mul(12, 0)
        copy_t("x", 7)
        mul(12, 1)
        mm2(12, 3)
        silu(12, 2)
        norm(8, 0)
        mm2(13, 0)
        silu(12, 3)
        mul(12, 2)
        mm2(13, 1)
        silu(13, 0)
        mul(12, 3)
        silu(13, 1)
        mm2(13, 2)
        mul(13, 0)
        silu(13, 2)
        mm2(13, 3)
        quant_t("x", 7)
        mul(13, 1)
        silu(13, 3)
        mm2(14, 0)
        mul(13, 2)
        silu(14, 0)
        mm2(14, 1)
        mul(13, 3)
        silu(14, 1)
        mm2(14, 2)
        mul(14, 0)
        silu(14, 2)
        mm2(14, 3)
        norm(8, 1)
        silu(14, 3)
        transpose_x(8)
        mul(14, 1)
        mm2(15, 0)
        mul(14, 2)
        copy_t("x", 8)
        mul(14, 3)
        mm2(15, 1)
        silu(15, 0)
        quant_t("x", 8)
        mm2(15, 2)
        silu(15, 1)
        mul(15, 0)
        mm2(15, 3)
        silu(15, 2)
        mul(15, 1)
        silu(15, 3)
        mm2(16, 0)
        mul(15, 2)
        silu(16, 0)
        mm2(16, 1)
        mul(15, 3)
        silu(16, 1)
        mm2(16, 2)
        mul(16, 0)
        silu(16, 2)
        mm2(16, 3)
        mul(16, 1)
        silu(16, 3)
        mm2(17, 0)
        mul(16, 2)
        silu(17, 0)
        mm2(17, 1)
        mul(16, 3)
        silu(17, 1)
        mm2(17, 2)
        mul(17, 0)
        silu(17, 2)
        mm2(17, 3)
        mul(17, 1)
        silu(17, 3)
        mul(17, 2)
        mul(17, 3)
